import numpy as np
import ml_dtypes


def mxq(x, axis, fmt="e4m3"):
    dtype, down = {"e4m3": (ml_dtypes.float8_e4m3fn, 7), "e5m2": (ml_dtypes.float8_e5m2, 14)}[fmt]
    v = np.moveaxis(np.asarray(x, np.float32).astype(ml_dtypes.bfloat16).astype(np.float64), axis, -1)
    blocks = v.reshape(v.shape[:-1] + (-1, 32))
    amax = np.abs(blocks).max(-1, keepdims=True)
    byte = np.maximum(np.where(amax > 0, np.frexp(amax)[1] - 1 + 127, 0) - down, 1)
    scale = np.exp2(byte - 127.0)
    codes = (blocks / scale).astype(np.float32).astype(dtype).astype(np.float64)
    return np.moveaxis((codes * scale).reshape(v.shape), -1, axis)


WIDE = False


def mx_kscale(k):
    if not WIDE:
        return np.ones(k)
    levels = np.array([10, -10, 5, -5, 0])
    a = np.random.permutation(np.resize(levels, k // 512 * 4)).reshape(k // 512, 4)
    idx = np.arange(k)
    return np.exp2(a[idx // 512, idx % 128 // 32])


BF16 = ml_dtypes.bfloat16


def bf(x):
    return np.asarray(x, np.float32).astype(BF16)


def f64(x):
    return np.asarray(x).astype(np.float64)


E2M1 = np.array([0.0, 0.5, 1.0, 1.5, 2.0, 3.0, 4.0, 6.0, -0.0, -0.5, -1.0, -1.5, -2.0, -3.0, -4.0, -6.0])


def pack_weight(w, fmt):
    k, n = w.shape
    w = f64(bf(w)).reshape(k // 32, 32, n)
    amax = np.abs(w).max(1)
    if fmt == "e4m3":
        byte = np.frexp(amax)[1] - 1 + 127 - 7
    else:
        mant, ex = np.frexp(amax / 6.0)
        byte = np.where(mant > 0.5, ex, ex - 1) + 127
    byte = np.clip(np.where(amax > 0, byte, 1), 1, 254)
    scaled = (w * np.exp2(127.0 - byte)[:, None, :]).reshape(k, n).astype(np.float32)
    by_word = np.ascontiguousarray(scaled.reshape(k // 512, 128, 4, n).transpose(0, 1, 3, 2))
    if fmt == "e4m3":
        words = by_word.astype(ml_dtypes.float8_e4m3fn).view(np.uint8)
    else:
        c = by_word.astype(ml_dtypes.float4_e2m1fn).view(np.uint8) & 0xF
        words = c[..., 0::2] | (c[..., 1::2] << 4)
    return np.ascontiguousarray(words), np.ascontiguousarray(byte.astype(np.uint8).reshape(k // 512, 16, n))


def unpack_weight(words, scales, fmt):
    g, p, n, _ = words.shape
    if fmt == "e4m3":
        vals = np.ascontiguousarray(words).view(ml_dtypes.float8_e4m3fn).astype(np.float64)
    else:
        nib = np.empty((g, p, n, 4), np.uint8)
        nib[..., 0::2] = words & 0xF
        nib[..., 1::2] = words >> 4
        vals = E2M1[nib]
    vals = vals * np.repeat(np.exp2(scales.astype(np.float64) - 127.0), 8, axis=1)[..., None]
    return vals.transpose(0, 1, 3, 2).reshape(g * 512, n)


M, K, N = 256, 4096, 4096


def setup_inputs():
    s = mx_kscale(K)
    x = bf(np.random.standard_normal((M, K)) * s)
    W = np.random.standard_normal((K, N)) * (1.0 / 64.0) / s[:, None]
    weight_words, weight_scales = pack_weight(W, "e4m3")
    bias = bf(np.random.standard_normal(N))
    return {"x": x, "weight_words": weight_words, "weight_scales": weight_scales, "bias": bias}


def reference(x, weight_words, weight_scales, bias):
    w = unpack_weight(weight_words, weight_scales, "e4m3")
    return (mxq(f64(x), 1, "e4m3") @ w) + f64(bias)

@@ -1,0 +1,173 @@
+from contextlib import ExitStack
+
+import concourse.mybir as mybir
+from concourse.masks import make_identity
+
+FLOPS = 2 * 256 * 4096 * 4096
+
+F32 = mybir.dt.float32
+BF16 = mybir.dt.bfloat16
+I32 = mybir.dt.int32
+U32 = mybir.dt.uint32
+U8 = mybir.dt.uint8
+FP8X4 = mybir.dt.float8_e4m3fn_x4
+
+P = 128
+M_TILES = 2
+GROUPS = 8
+N = 4096
+N_TILE = 512
+ROUND_COLS = 1024
+ROUNDS = N // ROUND_COLS
+TILES_PER_ROUND = ROUND_COLS // N_TILE
+
+
+def tile_fp8amperelinear_kernel(tc, x, weight_words, weight_scales, bias, out):
+    nc = tc.nc
+    with ExitStack() as ctx:
+        ctx.enter_context(tc.manual_schedule())
+        keep = ctx.enter_context(tc.tile_pool(name="keep", bufs=1))
+        psum = ctx.enter_context(tc.psum_pool(name="psum", bufs=8))
+
+        bias8 = keep.tile([P, N_TILE], BF16, name="bias8")
+        nc.vector.memset(bias8[:], 0.0)
+        wplane = [keep.tile([P, N], U8, name="wplane%d" % h, align_bytes=64) for h in range(2)]
+        for h in range(2):
+            nc.vector.memset(wplane[h][:].bitcast(I32), 0)
+        ident_b = keep.tile([P, P], BF16, name="ident_b")
+        make_identity(nc, ident_b[:])
+        ident_f = keep.tile([P, P], F32, name="ident_f")
+        make_identity(nc, ident_f[:])
+
+        nc.scalar.dma_start(out=bias8[0:8, :], in_=bias.rearrange("(j c) -> j c", j=8))
+
+        x_sb = [[None, None], [None, None]]
+        for kh in range(2):
+            for mt in range(M_TILES):
+                t = keep.tile([P, 2048], BF16, name="x_sb_%d_%d" % (mt, kh))
+                nc.sync.dma_start(
+                    out=t[:], in_=x[P * mt : P * (mt + 1), 2048 * kh : 2048 * (kh + 1)]
+                )
+                x_sb[mt][kh] = t
+
+        for h in range(2):
+            for q in range(4):
+                nc.sync.dma_start(
+                    out=wplane[h][32 * q : 32 * q + 16, :].bitcast(I32),
+                    in_=weight_scales[4 * h : 4 * h + 4, 4 * q : 4 * q + 4, :].bitcast(I32),
+                )
+
+        ww = weight_words.rearrange("g p n t -> g p (n t)")
+        w_sb = []
+        for r in range(ROUNDS):
+            row = []
+            for g in range(GROUPS):
+                t = keep.tile([P, ROUND_COLS], U32, name="w_sb_%d_%d" % (r, g), align_bytes=64)
+                nc.sync.dma_start(
+                    out=t[:].bitcast(I32),
+                    in_=ww[g, :, 4 * ROUND_COLS * r : 4 * ROUND_COLS * (r + 1)].bitcast(I32),
+                )
+                row.append(t)
+            w_sb.append(row)
+
+        bias_bc = keep.tile([P, N], BF16, name="bias_bc")
+        for j in range(8):
+            pb = psum.tile([P, N_TILE], F32, name="pb", tag="bank")
+            nc.tensor.matmul(
+                pb[:],
+                lhsT=ident_b[:, j : j + 1].to_broadcast([P, P]),
+                rhs=bias8[:],
+                start=True,
+                stop=True,
+            )
+            dst = bias_bc[:, N_TILE * j : N_TILE * (j + 1)]
+            if j % 2 == 0:
+                nc.vector.tensor_copy(out=dst, in_=pb[:])
+            else:
+                nc.scalar.copy(out=dst, in_=pb[:])
+
+        xcodes = keep.tile([P, GROUPS, 256], U32, name="xcodes", align_bytes=64)
+        xplane = keep.tile([P, GROUPS, 256], U8, name="xplane", align_bytes=64)
+        grouped = [
+            keep.tile([P, 2048], BF16, name="grouped%d" % j, align_bytes=64) for j in range(4)
+        ]
+
+        def quantise_pair(j):
+            nc.vector.quantize_mx(
+                out=xcodes[:, 2 * j : 2 * j + 2, :].rearrange("p g m -> p (g m)").bitcast(FP8X4),
+                scales=xplane[:, 2 * j : 2 * j + 2, :].rearrange("p g m -> p (g m)"),
+                in_=grouped[j][:],
+            )
+
+        for g in range(GROUPS):
+            kh, gl = g // 4, g % 4
+            xt = psum.tile([P, 2, 256], F32, name="xt", tag="bank")
+            for mt in range(M_TILES):
+                words = x_sb[mt][kh][:].bitcast(F32)
+                for u in range(2):
+                    nc.tensor.transpose(
+                        xt[:, u, P * mt : P * (mt + 1)],
+                        words[:, 256 * gl + u : 256 * (gl + 1) : 2],
+                        ident_f[:],
+                    )
+            dst = (
+                grouped[g // 2][:, 1024 * (g % 2) : 1024 * (g % 2 + 1)]
+                .bitcast(F32)
+                .rearrange("p (m u) -> p m u", u=2)
+            )
+            src = xt[:].rearrange("p u m -> p m u")
+            if g % 2 == 0:
+                nc.vector.tensor_copy(out=dst, in_=src)
+                if g >= 2:
+                    quantise_pair(g // 2 - 1)
+            else:
+                nc.scalar.copy(out=dst, in_=src)
+        quantise_pair(3)
+
+        out_sb = {}
+        for mt in range(M_TILES):
+            out_sb[(mt, 0)] = keep.tile([P, 2048], F32, name="out_sb_%d_0" % mt)
+            out_sb[(mt, 2)] = keep.tile([P, 1024], F32, name="out_sb_%d_2" % mt)
+            out_sb[(mt, 3)] = keep.tile([P, 1024], F32, name="out_sb_%d_3" % mt)
+
+        for r in range(ROUNDS):
+            acc = {}
+            for nt in range(TILES_PER_ROUND):
+                for mt in range(M_TILES):
+                    acc[(nt, mt)] = psum.tile([P, N_TILE], F32, name="acc", tag="bank")
+            for g in range(GROUPS):
+                h, k = g // 4, g % 4
+                for nt in range(TILES_PER_ROUND):
+                    n0 = ROUND_COLS * r + N_TILE * nt
+                    for mt in range(M_TILES):
+                        nc.tensor.matmul_mx(
+                            out=acc[(nt, mt)][:],
+                            lhsT=xcodes[:, g, P * mt : P * (mt + 1)].bitcast(FP8X4),
+                            lhsT_scale=xplane[:, g, P * mt : P * (mt + 1)],
+                            rhs=w_sb[r][g][:, N_TILE * nt : N_TILE * (nt + 1)].bitcast(FP8X4),
+                            rhs_scale=wplane[h][4 * k : P, n0 : n0 + N_TILE],
+                            start=(g == 0),
+                            stop=(g == GROUPS - 1),
+                        )
+            for nt in range(TILES_PER_ROUND):
+                n0 = ROUND_COLS * r + N_TILE * nt
+                for mt in range(M_TILES):
+                    if r < 2:
+                        dst = out_sb[(mt, 0)][:, n0 : n0 + N_TILE]
+                    else:
+                        dst = out_sb[(mt, r)][:, N_TILE * nt : N_TILE * (nt + 1)]
+                    nc.vector.tensor_tensor(
+                        out=dst,
+                        in0=acc[(nt, mt)][:],
+                        in1=bias_bc[:, n0 : n0 + N_TILE],
+                        op=mybir.AluOpType.add,
+                    )
+
+        for mt in range(M_TILES):
+            nc.sync.dma_start(out=out[P * mt : P * (mt + 1), 0:2048], in_=out_sb[(mt, 0)][:])
+        for r in (2, 3):
+            for mt in range(M_TILES):
+                nc.sync.dma_start(
+                    out=out[P * mt : P * (mt + 1), ROUND_COLS * r : ROUND_COLS * (r + 1)],
+                    in_=out_sb[(mt, r)][:],
+                )

@@ -52,9 +52,9 @@ def tile_fp8amperelinear_kernel(tc, x, weight_words, weight_scales, bias, out):
 
         for h in range(2):
             for q in range(4):
-                nc.sync.dma_start(
-                    out=wplane[h][32 * q : 32 * q + 16, :].bitcast(I32),
-                    in_=weight_scales[4 * h : 4 * h + 4, 4 * q : 4 * q + 4, :].bitcast(I32),
+                nc.gpsimd.dma_start(
+                    out=wplane[h][32 * q : 32 * q + 16, :].bitcast(F32),
+                    in_=weight_scales[4 * h : 4 * h + 4, 4 * q : 4 * q + 4, :].bitcast(F32),
                 )
 
         ww = weight_words.rearrange("g p n t -> g p (n t)")

@@ -11,15 +11,18 @@ I32 = mybir.dt.int32
 U32 = mybir.dt.uint32
 U8 = mybir.dt.uint8
 FP8X4 = mybir.dt.float8_e4m3fn_x4
+ADD = mybir.AluOpType.add
 
 P = 128
 M_TILES = 2
 GROUPS = 8
+K = 4096
 N = 4096
 N_TILE = 512
-ROUND_COLS = 1024
+ROUND_COLS = 2048
 ROUNDS = N // ROUND_COLS
-TILES_PER_ROUND = ROUND_COLS // N_TILE
+
+BANKS = [(0, 0), (1, 0), (0, 1), (1, 1), (2, 0), (3, 0), (2, 1), (3, 1)]
 
 
 def tile_fp8amperelinear_kernel(tc, x, weight_words, weight_scales, bias, out):
@@ -29,8 +32,6 @@ def tile_fp8amperelinear_kernel(tc, x, weight_words, weight_scales, bias, out):
         keep = ctx.enter_context(tc.tile_pool(name="keep", bufs=1))
         psum = ctx.enter_context(tc.psum_pool(name="psum", bufs=8))
 
-        bias8 = keep.tile([P, N_TILE], BF16, name="bias8")
-        nc.vector.memset(bias8[:], 0.0)
         wplane = [keep.tile([P, N], U8, name="wplane%d" % h, align_bytes=64) for h in range(2)]
         for h in range(2):
             nc.vector.memset(wplane[h][:].bitcast(I32), 0)
@@ -39,16 +40,17 @@ def tile_fp8amperelinear_kernel(tc, x, weight_words, weight_scales, bias, out):
         ident_f = keep.tile([P, P], F32, name="ident_f")
         make_identity(nc, ident_f[:])
 
-        nc.scalar.dma_start(out=bias8[0:8, :], in_=bias.rearrange("(j c) -> j c", j=8))
+        bias8 = keep.tile([P, N_TILE], BF16, name="bias8")
+        nc.scalar.dma_start(
+            out=bias8[:],
+            in_=bias.rearrange("(o j c) -> o j c", o=1, j=8).to_broadcast([16, 8, N_TILE]),
+        )
 
-        x_sb = [[None, None], [None, None]]
-        for kh in range(2):
-            for mt in range(M_TILES):
-                t = keep.tile([P, 2048], BF16, name="x_sb_%d_%d" % (mt, kh))
-                nc.sync.dma_start(
-                    out=t[:], in_=x[P * mt : P * (mt + 1), 2048 * kh : 2048 * (kh + 1)]
-                )
-                x_sb[mt][kh] = t
+        x_sb = []
+        for mt in range(M_TILES):
+            t = keep.tile([P, K], BF16, name="x_sb_%d" % mt)
+            nc.sync.dma_start(out=t[:], in_=x[P * mt : P * (mt + 1), :])
+            x_sb.append(t)
 
         for h in range(2):
             for q in range(4):
@@ -99,23 +101,23 @@ def tile_fp8amperelinear_kernel(tc, x, weight_words, weight_scales, bias, out):
                 in_=grouped[j][:],
             )
 
-        for g in range(GROUPS):
-            kh, gl = g // 4, g % 4
-            xt = psum.tile([P, 2, 256], F32, name="xt", tag="bank")
-            for mt in range(M_TILES):
-                words = x_sb[mt][kh][:].bitcast(F32)
+        xt = [psum.tile([P, 2, 256], F32, name="xt%d" % g, tag="bank") for g in range(GROUPS)]
+        for mt in range(M_TILES):
+            words = x_sb[mt][:].bitcast(F32)
+            for g in range(GROUPS):
                 for u in range(2):
                     nc.tensor.transpose(
-                        xt[:, u, P * mt : P * (mt + 1)],
-                        words[:, 256 * gl + u : 256 * (gl + 1) : 2],
+                        xt[g][:, u, P * mt : P * (mt + 1)],
+                        words[:, 256 * g + u : 256 * (g + 1) : 2],
                         ident_f[:],
                     )
+        for g in range(GROUPS):
             dst = (
                 grouped[g // 2][:, 1024 * (g % 2) : 1024 * (g % 2 + 1)]
                 .bitcast(F32)
                 .rearrange("p (m u) -> p m u", u=2)
             )
-            src = xt[:].rearrange("p u m -> p m u")
+            src = xt[g][:].rearrange("p u m -> p m u")
             if g % 2 == 0:
                 nc.vector.tensor_copy(out=dst, in_=src)
                 if g >= 2:
@@ -126,48 +128,53 @@ def tile_fp8amperelinear_kernel(tc, x, weight_words, weight_scales, bias, out):
 
         out_sb = {}
         for mt in range(M_TILES):
-            out_sb[(mt, 0)] = keep.tile([P, 2048], F32, name="out_sb_%d_0" % mt)
-            out_sb[(mt, 2)] = keep.tile([P, 1024], F32, name="out_sb_%d_2" % mt)
-            out_sb[(mt, 3)] = keep.tile([P, 1024], F32, name="out_sb_%d_3" % mt)
+            out_sb[(0, mt, 0)] = keep.tile([P, 2048], F32, name="out_sb_0_%d" % mt)
+            for half in range(2):
+                out_sb[(1, mt, half)] = keep.tile([P, 1024], F32, name="out_sb_1_%d_%d" % (mt, half))
+
+        def out_slice(r, nt, mt):
+            if r == 0:
+                return out_sb[(0, mt, 0)][:, N_TILE * nt : N_TILE * (nt + 1)]
+            return out_sb[(1, mt, nt // 2)][:, N_TILE * (nt % 2) : N_TILE * (nt % 2 + 1)]
 
         for r in range(ROUNDS):
             acc = {}
-            for nt in range(TILES_PER_ROUND):
-                for mt in range(M_TILES):
-                    acc[(nt, mt)] = psum.tile([P, N_TILE], F32, name="acc", tag="bank")
+            for b in BANKS:
+                acc[b] = psum.tile([P, N_TILE], F32, name="acc", tag="bank")
             for g in range(GROUPS):
                 h, k = g // 4, g % 4
-                for nt in range(TILES_PER_ROUND):
+                for nt, mt in BANKS:
                     n0 = ROUND_COLS * r + N_TILE * nt
-                    for mt in range(M_TILES):
-                        nc.tensor.matmul_mx(
-                            out=acc[(nt, mt)][:],
-                            lhsT=xcodes[:, g, P * mt : P * (mt + 1)].bitcast(FP8X4),
-                            lhsT_scale=xplane[:, g, P * mt : P * (mt + 1)],
-                            rhs=w_sb[r][g][:, N_TILE * nt : N_TILE * (nt + 1)].bitcast(FP8X4),
-                            rhs_scale=wplane[h][4 * k : P, n0 : n0 + N_TILE],
-                            start=(g == 0),
-                            stop=(g == GROUPS - 1),
-                        )
-            for nt in range(TILES_PER_ROUND):
-                n0 = ROUND_COLS * r + N_TILE * nt
-                for mt in range(M_TILES):
-                    if r < 2:
-                        dst = out_sb[(mt, 0)][:, n0 : n0 + N_TILE]
-                    else:
-                        dst = out_sb[(mt, r)][:, N_TILE * nt : N_TILE * (nt + 1)]
-                    nc.vector.tensor_tensor(
-                        out=dst,
-                        in0=acc[(nt, mt)][:],
-                        in1=bias_bc[:, n0 : n0 + N_TILE],
-                        op=mybir.AluOpType.add,
+                    nc.tensor.matmul_mx(
+                        out=acc[(nt, mt)][:],
+                        lhsT=xcodes[:, g, P * mt : P * (mt + 1)].bitcast(FP8X4),
+                        lhsT_scale=xplane[:, g, P * mt : P * (mt + 1)],
+                        rhs=w_sb[r][g][:, N_TILE * nt : N_TILE * (nt + 1)].bitcast(FP8X4),
+                        rhs_scale=wplane[h][4 * k : P, n0 : n0 + N_TILE],
+                        start=(g == 0),
+                        stop=(g == GROUPS - 1),
                     )
+            later = []
+            for i, (nt, mt) in enumerate(BANKS):
+                n0 = ROUND_COLS * r + N_TILE * nt
+                dst = out_slice(r, nt, mt)
+                if r == 0 and i % 2 == 1:
+                    nc.scalar.copy(out=dst, in_=acc[(nt, mt)][:])
+                    later.append((dst, n0))
+                else:
+                    nc.vector.tensor_tensor(
+                        out=dst, in0=acc[(nt, mt)][:], in1=bias_bc[:, n0 : n0 + N_TILE], op=ADD
+                    )
+            for dst, n0 in later:
+                nc.vector.tensor_tensor(
+                    out=dst, in0=dst, in1=bias_bc[:, n0 : n0 + N_TILE], op=ADD
+                )
 
         for mt in range(M_TILES):
-            nc.sync.dma_start(out=out[P * mt : P * (mt + 1), 0:2048], in_=out_sb[(mt, 0)][:])
-        for r in (2, 3):
+            nc.sync.dma_start(out=out[P * mt : P * (mt + 1), 0:2048], in_=out_sb[(0, mt, 0)][:])
+        for half in range(2):
             for mt in range(M_TILES):
+                c0 = 2048 + 1024 * half
                 nc.sync.dma_start(
-                    out=out[P * mt : P * (mt + 1), ROUND_COLS * r : ROUND_COLS * (r + 1)],
-                    in_=out_sb[(mt, r)][:],
+                    out=out[P * mt : P * (mt + 1), c0 : c0 + 1024], in_=out_sb[(1, mt, half)][:]
                 )

@@ -21,6 +21,7 @@ N = 4096
 N_TILE = 512
 ROUND_COLS = 2048
 ROUNDS = N // ROUND_COLS
+PAD = 48
 
 BANKS = [(0, 0), (1, 0), (0, 1), (1, 1), (2, 0), (3, 0), (2, 1), (3, 1)]
 
@@ -32,13 +33,13 @@ def tile_fp8amperelinear_kernel(tc, x, weight_words, weight_scales, bias, out):
         keep = ctx.enter_context(tc.tile_pool(name="keep", bufs=1))
         psum = ctx.enter_context(tc.psum_pool(name="psum", bufs=8))
 
-        wplane = [keep.tile([P, N], U8, name="wplane%d" % h, align_bytes=64) for h in range(2)]
+        wplane = [keep.tile([P, N], U8, name="wplane%d" % h, align_bytes=256) for h in range(2)]
         for h in range(2):
             nc.vector.memset(wplane[h][:].bitcast(I32), 0)
-        ident_b = keep.tile([P, P], BF16, name="ident_b")
-        make_identity(nc, ident_b[:])
         ident_f = keep.tile([P, P], F32, name="ident_f")
         make_identity(nc, ident_f[:])
+        ident_b = keep.tile([P, P], BF16, name="ident_b")
+        make_identity(nc, ident_b[:])
 
         bias8 = keep.tile([P, N_TILE], BF16, name="bias8")
         nc.scalar.dma_start(
@@ -46,11 +47,14 @@ def tile_fp8amperelinear_kernel(tc, x, weight_words, weight_scales, bias, out):
             in_=bias.rearrange("(o j c) -> o j c", o=1, j=8).to_broadcast([16, 8, N_TILE]),
         )
 
-        x_sb = []
-        for mt in range(M_TILES):
-            t = keep.tile([P, K], BF16, name="x_sb_%d" % mt)
-            nc.sync.dma_start(out=t[:], in_=x[P * mt : P * (mt + 1), :])
-            x_sb.append(t)
+        x_sb = [[None, None], [None, None]]
+        for kh in range(2):
+            for mt in range(M_TILES):
+                t = keep.tile([P, 2048], BF16, name="x_sb_%d_%d" % (mt, kh))
+                nc.sync.dma_start(
+                    out=t[:], in_=x[P * mt : P * (mt + 1), 2048 * kh : 2048 * (kh + 1)]
+                )
+                x_sb[mt][kh] = t
 
         for h in range(2):
             for q in range(4):
@@ -64,7 +68,7 @@ def tile_fp8amperelinear_kernel(tc, x, weight_words, weight_scales, bias, out):
         for r in range(ROUNDS):
             row = []
             for g in range(GROUPS):
-                t = keep.tile([P, ROUND_COLS], U32, name="w_sb_%d_%d" % (r, g), align_bytes=64)
+                t = keep.tile([P, ROUND_COLS], U32, name="w_sb_%d_%d" % (r, g), align_bytes=256)
                 nc.sync.dma_start(
                     out=t[:].bitcast(I32),
                     in_=ww[g, :, 4 * ROUND_COLS * r : 4 * ROUND_COLS * (r + 1)].bitcast(I32),
@@ -73,108 +77,142 @@ def tile_fp8amperelinear_kernel(tc, x, weight_words, weight_scales, bias, out):
             w_sb.append(row)
 
         bias_bc = keep.tile([P, N], BF16, name="bias_bc")
-        for j in range(8):
-            pb = psum.tile([P, N_TILE], F32, name="pb", tag="bank")
-            nc.tensor.matmul(
-                pb[:],
-                lhsT=ident_b[:, j : j + 1].to_broadcast([P, P]),
-                rhs=bias8[:],
-                start=True,
-                stop=True,
-            )
-            dst = bias_bc[:, N_TILE * j : N_TILE * (j + 1)]
-            if j % 2 == 0:
-                nc.vector.tensor_copy(out=dst, in_=pb[:])
-            else:
-                nc.scalar.copy(out=dst, in_=pb[:])
-
-        xcodes = keep.tile([P, GROUPS, 256], U32, name="xcodes", align_bytes=64)
-        xplane = keep.tile([P, GROUPS, 256], U8, name="xplane", align_bytes=64)
+        xcodes = keep.tile([P, PAD + GROUPS * 256], U32, name="xcodes", align_bytes=256)
+        xplane = keep.tile([P, 2 * GROUPS, 256], U8, name="xplane", align_bytes=256)
         grouped = [
             keep.tile([P, 2048], BF16, name="grouped%d" % j, align_bytes=64) for j in range(4)
         ]
 
-        def quantise_pair(j):
-            nc.vector.quantize_mx(
-                out=xcodes[:, 2 * j : 2 * j + 2, :].rearrange("p g m -> p (g m)").bitcast(FP8X4),
-                scales=xplane[:, 2 * j : 2 * j + 2, :].rearrange("p g m -> p (g m)"),
-                in_=grouped[j][:],
-            )
+        def codes_of(g, mt):
+            o = PAD + 256 * g + P * mt
+            return xcodes[:, o : o + P].bitcast(FP8X4)
 
-        xt = [psum.tile([P, 2, 256], F32, name="xt%d" % g, tag="bank") for g in range(GROUPS)]
-        for mt in range(M_TILES):
-            words = x_sb[mt][:].bitcast(F32)
-            for g in range(GROUPS):
-                for u in range(2):
-                    nc.tensor.transpose(
-                        xt[g][:, u, P * mt : P * (mt + 1)],
-                        words[:, 256 * g + u : 256 * (g + 1) : 2],
-                        ident_f[:],
-                    )
-        for g in range(GROUPS):
+        def plane_of(g, mt):
+            return xplane[:, 2 * g + mt, 0:P]
+
+        def quantise(g):
+            for mt in range(M_TILES):
+                o = 1024 * (g % 2) + 512 * mt
+                nc.vector.quantize_mx(
+                    out=codes_of(g, mt), scales=plane_of(g, mt), in_=grouped[g // 2][:, o : o + 512]
+                )
+
+        def spread_bias(i):
+            pb = psum.tile([P, 1024], BF16, name="pb", tag="bank")
+            for e in range(2):
+                j = 2 * i + e
+                nc.tensor.matmul(
+                    pb[:, N_TILE * e : N_TILE * (e + 1)],
+                    lhsT=ident_b[:, j : j + 1].to_broadcast([P, P]),
+                    rhs=bias8[:],
+                    start=True,
+                    stop=True,
+                )
+            return pb
+
+        def bias_out(i, pb):
+            nc.scalar.copy(out=bias_bc[:, 1024 * i : 1024 * (i + 1)], in_=pb[:])
+
+        def regroup(g, xt, engine_copy):
             dst = (
                 grouped[g // 2][:, 1024 * (g % 2) : 1024 * (g % 2 + 1)]
                 .bitcast(F32)
                 .rearrange("p (m u) -> p m u", u=2)
             )
-            src = xt[g][:].rearrange("p u m -> p m u")
-            if g % 2 == 0:
-                nc.vector.tensor_copy(out=dst, in_=src)
-                if g >= 2:
-                    quantise_pair(g // 2 - 1)
-            else:
-                nc.scalar.copy(out=dst, in_=src)
-        quantise_pair(3)
+            engine_copy(out=dst, in_=xt[:].rearrange("p u m -> p m u"))
 
-        out_sb = {}
-        for mt in range(M_TILES):
-            out_sb[(0, mt, 0)] = keep.tile([P, 2048], F32, name="out_sb_0_%d" % mt)
-            for half in range(2):
-                out_sb[(1, mt, half)] = keep.tile([P, 1024], F32, name="out_sb_1_%d_%d" % (mt, half))
-
-        def out_slice(r, nt, mt):
-            if r == 0:
-                return out_sb[(0, mt, 0)][:, N_TILE * nt : N_TILE * (nt + 1)]
-            return out_sb[(1, mt, nt // 2)][:, N_TILE * (nt % 2) : N_TILE * (nt % 2 + 1)]
-
-        for r in range(ROUNDS):
-            acc = {}
-            for b in BANKS:
-                acc[b] = psum.tile([P, N_TILE], F32, name="acc", tag="bank")
-            for g in range(GROUPS):
-                h, k = g // 4, g % 4
-                for nt, mt in BANKS:
-                    n0 = ROUND_COLS * r + N_TILE * nt
-                    nc.tensor.matmul_mx(
-                        out=acc[(nt, mt)][:],
-                        lhsT=xcodes[:, g, P * mt : P * (mt + 1)].bitcast(FP8X4),
-                        lhsT_scale=xplane[:, g, P * mt : P * (mt + 1)],
-                        rhs=w_sb[r][g][:, N_TILE * nt : N_TILE * (nt + 1)].bitcast(FP8X4),
-                        rhs_scale=wplane[h][4 * k : P, n0 : n0 + N_TILE],
-                        start=(g == 0),
-                        stop=(g == GROUPS - 1),
-                    )
-            later = []
-            for i, (nt, mt) in enumerate(BANKS):
-                n0 = ROUND_COLS * r + N_TILE * nt
-                dst = out_slice(r, nt, mt)
-                if r == 0 and i % 2 == 1:
-                    nc.scalar.copy(out=dst, in_=acc[(nt, mt)][:])
-                    later.append((dst, n0))
-                else:
-                    nc.vector.tensor_tensor(
-                        out=dst, in0=acc[(nt, mt)][:], in1=bias_bc[:, n0 : n0 + N_TILE], op=ADD
-                    )
-            for dst, n0 in later:
-                nc.vector.tensor_tensor(
-                    out=dst, in0=dst, in1=bias_bc[:, n0 : n0 + N_TILE], op=ADD
-                )
-
-        for mt in range(M_TILES):
-            nc.sync.dma_start(out=out[P * mt : P * (mt + 1), 0:2048], in_=out_sb[(0, mt, 0)][:])
-        for half in range(2):
+        for kh in range(2):
+            xt = [
+                psum.tile([P, 2, 256], F32, name="xt%d" % (4 * kh + gl), tag="bank")
+                for gl in range(4)
+            ]
+            pbs = []
             for mt in range(M_TILES):
-                c0 = 2048 + 1024 * half
-                nc.sync.dma_start(
-                    out=out[P * mt : P * (mt + 1), c0 : c0 + 1024], in_=out_sb[(1, mt, half)][:]
-                )
+                words = x_sb[mt][kh][:].bitcast(F32)
+                for gl in range(4):
+                    for u in range(2):
+                        nc.tensor.transpose(
+                            xt[gl][:, u, P * mt : P * (mt + 1)],
+                            words[:, 256 * gl + u : 256 * (gl + 1) : 2],
+                            ident_f[:],
+                        )
+                pbs.append(spread_bias(2 * kh + mt))
+            g0 = 4 * kh
+            bias_out(2 * kh, pbs[0])
+            regroup(g0 + 0, xt[0], nc.vector.tensor_copy)
+            regroup(g0 + 1, xt[1], nc.scalar.copy)
+            regroup(g0 + 2, xt[2], nc.vector.tensor_copy)
+            regroup(g0 + 3, xt[3], nc.scalar.copy)
+            bias_out(2 * kh + 1, pbs[1])
+            for gl in range(4):
+                quantise(g0 + gl)
+
+        out_a = [keep.tile([P, 2048], F32, name="out_a_%d" % mt) for mt in range(M_TILES)]
+        out_b = {}
+        for pair in range(3):
+            out_b[pair] = keep.tile([P, 1024], F32, name="out_b_%d" % pair)
+        out_b[3] = keep.tile([P, N_TILE], F32, name="out_b_3")
+        out_b[4] = keep.tile([P, N_TILE], F32, name="out_b_4")
+
+        def out_slice(r, i):
+            nt, mt = BANKS[i]
+            if r == 0:
+                return out_a[mt][:, N_TILE * nt : N_TILE * (nt + 1)]
+            if i < 6:
+                return out_b[i // 2][:, N_TILE * (i % 2) : N_TILE * (i % 2 + 1)]
+            return out_b[i - 3][:]
+
+        def mx_pass(r, g, acc, nt, mt):
+            h, k = g // 4, g % 4
+            n0 = ROUND_COLS * r + N_TILE * nt
+            nc.tensor.matmul_mx(
+                out=acc[(nt, mt)][:],
+                lhsT=codes_of(g, mt),
+                lhsT_scale=plane_of(g, mt),
+                rhs=w_sb[r][g][:, N_TILE * nt : N_TILE * (nt + 1)].bitcast(FP8X4),
+                rhs_scale=wplane[h][4 * k : P, n0 : n0 + N_TILE],
+                start=(g == 0),
+                stop=(g == GROUPS - 1),
+            )
+
+        def add_bias(dst, src, n0):
+            nc.vector.tensor_tensor(out=dst, in0=src, in1=bias_bc[:, n0 : n0 + N_TILE], op=ADD)
+
+        acc = {}
+        for b in BANKS:
+            acc[b] = psum.tile([P, N_TILE], F32, name="acc", tag="bank")
+        for g in range(GROUPS):
+            for nt, mt in BANKS:
+                mx_pass(0, g, acc, nt, mt)
+        later = []
+        for i, (nt, mt) in enumerate(BANKS):
+            dst = out_slice(0, i)
+            if i % 2 == 1:
+                nc.scalar.copy(out=dst, in_=acc[(nt, mt)][:])
+                later.append((dst, N_TILE * nt))
+            else:
+                add_bias(dst, acc[(nt, mt)][:], N_TILE * nt)
+        for dst, n0 in later:
+            add_bias(dst, dst, n0)
+
+        acc = {}
+        for b in BANKS:
+            acc[b] = psum.tile([P, N_TILE], F32, name="acc", tag="bank")
+        for g in range(GROUPS - 2):
+            for nt, mt in BANKS:
+                mx_pass(1, g, acc, nt, mt)
+        for i, (nt, mt) in enumerate(BANKS):
+            mx_pass(1, GROUPS - 2, acc, nt, mt)
+            mx_pass(1, GROUPS - 1, acc, nt, mt)
+            add_bias(out_slice(1, i), acc[(nt, mt)][:], ROUND_COLS + N_TILE * nt)
+
+        for mt in range(M_TILES):
+            nc.sync.dma_start(out=out[P * mt : P * (mt + 1), 0:2048], in_=out_a[mt][:])
+        for pair in range(3):
+            nt, mt = BANKS[2 * pair]
+            c0 = ROUND_COLS + N_TILE * nt
+            nc.sync.dma_start(out=out[P * mt : P * (mt + 1), c0 : c0 + 1024], in_=out_b[pair][:])
+        for i in (6, 7):
+            nt, mt = BANKS[i]
+            c0 = ROUND_COLS + N_TILE * nt
+            nc.sync.dma_start(out=out[P * mt : P * (mt + 1), c0 : c0 + N_TILE], in_=out_b[i - 3][:])

@@ -20,10 +20,11 @@ K = 4096
 N = 4096
 N_TILE = 512
 ROUND_COLS = 2048
-ROUNDS = N // ROUND_COLS
 PAD = 48
 
-BANKS = [(0, 0), (1, 0), (0, 1), (1, 1), (2, 0), (3, 0), (2, 1), (3, 1)]
+BANKS_A = [(0, 0), (1, 0), (0, 1), (1, 1), (2, 0), (3, 0), (2, 1), (3, 1)]
+BANKS_B = [(0, 0), (1, 0), (0, 1), (1, 1), (2, 0), (2, 1), (3, 0), (3, 1)]
+TAPER = [(0, 2), (2, 1), (3, 1)]
 
 
 def tile_fp8amperelinear_kernel(tc, x, weight_words, weight_scales, bias, out):
@@ -51,9 +52,13 @@ def tile_fp8amperelinear_kernel(tc, x, weight_words, weight_scales, bias, out):
         for kh in range(2):
             for mt in range(M_TILES):
                 t = keep.tile([P, 2048], BF16, name="x_sb_%d_%d" % (mt, kh))
-                nc.sync.dma_start(
-                    out=t[:], in_=x[P * mt : P * (mt + 1), 2048 * kh : 2048 * (kh + 1)]
-                )
+                cuts = 2 if (kh, mt) == (0, 0) else 1
+                w = 2048 // cuts
+                for c in range(cuts):
+                    nc.sync.dma_start(
+                        out=t[:, w * c : w * (c + 1)],
+                        in_=x[P * mt : P * (mt + 1), 2048 * kh + w * c : 2048 * kh + w * (c + 1)],
+                    )
                 x_sb[mt][kh] = t
 
         for h in range(2):
@@ -64,17 +69,26 @@ def tile_fp8amperelinear_kernel(tc, x, weight_words, weight_scales, bias, out):
                 )
 
         ww = weight_words.rearrange("g p n t -> g p (n t)")
-        w_sb = []
-        for r in range(ROUNDS):
-            row = []
-            for g in range(GROUPS):
-                t = keep.tile([P, ROUND_COLS], U32, name="w_sb_%d_%d" % (r, g), align_bytes=256)
-                nc.sync.dma_start(
-                    out=t[:].bitcast(I32),
-                    in_=ww[g, :, 4 * ROUND_COLS * r : 4 * ROUND_COLS * (r + 1)].bitcast(I32),
-                )
-                row.append(t)
-            w_sb.append(row)
+        w_sb = {}
+
+        def load_w(r, g, first, count):
+            t = keep.tile(
+                [P, N_TILE * count], U32, name="w_sb_%d_%d_%d" % (r, g, first), align_bytes=256
+            )
+            c0 = 4 * (ROUND_COLS * r + N_TILE * first)
+            nc.sync.dma_start(
+                out=t[:].bitcast(I32), in_=ww[g, :, c0 : c0 + 4 * N_TILE * count].bitcast(I32)
+            )
+            for i in range(count):
+                w_sb[(r, g, first + i)] = (t, N_TILE * i)
+
+        for g in range(GROUPS):
+            load_w(0, g, 0, 4)
+        for g in range(GROUPS - 2):
+            load_w(1, g, 0, 4)
+        for first, count in TAPER:
+            for g in (GROUPS - 2, GROUPS - 1):
+                load_w(1, g, first, count)
 
         bias_bc = keep.tile([P, N], BF16, name="bias_bc")
         xcodes = keep.tile([P, PAD + GROUPS * 256], U32, name="xcodes", align_bytes=256)
@@ -148,28 +162,18 @@ def tile_fp8amperelinear_kernel(tc, x, weight_words, weight_scales, bias, out):
                 quantise(g0 + gl)
 
         out_a = [keep.tile([P, 2048], F32, name="out_a_%d" % mt) for mt in range(M_TILES)]
-        out_b = {}
-        for pair in range(3):
-            out_b[pair] = keep.tile([P, 1024], F32, name="out_b_%d" % pair)
-        out_b[3] = keep.tile([P, N_TILE], F32, name="out_b_3")
-        out_b[4] = keep.tile([P, N_TILE], F32, name="out_b_4")
-
-        def out_slice(r, i):
-            nt, mt = BANKS[i]
-            if r == 0:
-                return out_a[mt][:, N_TILE * nt : N_TILE * (nt + 1)]
-            if i < 6:
-                return out_b[i // 2][:, N_TILE * (i % 2) : N_TILE * (i % 2 + 1)]
-            return out_b[i - 3][:]
+        out_b = [keep.tile([P, 1024], F32, name="out_b_%d" % i) for i in range(2)]
+        out_b.extend([keep.tile([P, N_TILE], F32, name="out_b_%d" % i) for i in range(2, 6)])
 
         def mx_pass(r, g, acc, nt, mt):
             h, k = g // 4, g % 4
             n0 = ROUND_COLS * r + N_TILE * nt
+            t, c = w_sb[(r, g, nt)]
             nc.tensor.matmul_mx(
                 out=acc[(nt, mt)][:],
                 lhsT=codes_of(g, mt),
                 lhsT_scale=plane_of(g, mt),
-                rhs=w_sb[r][g][:, N_TILE * nt : N_TILE * (nt + 1)].bitcast(FP8X4),
+                rhs=t[:, c : c + N_TILE].bitcast(FP8X4),
                 rhs_scale=wplane[h][4 * k : P, n0 : n0 + N_TILE],
                 start=(g == 0),
                 stop=(g == GROUPS - 1),
@@ -179,14 +183,14 @@ def tile_fp8amperelinear_kernel(tc, x, weight_words, weight_scales, bias, out):
             nc.vector.tensor_tensor(out=dst, in0=src, in1=bias_bc[:, n0 : n0 + N_TILE], op=ADD)
 
         acc = {}
-        for b in BANKS:
+        for b in BANKS_A:
             acc[b] = psum.tile([P, N_TILE], F32, name="acc", tag="bank")
         for g in range(GROUPS):
-            for nt, mt in BANKS:
+            for nt, mt in BANKS_A:
                 mx_pass(0, g, acc, nt, mt)
         later = []
-        for i, (nt, mt) in enumerate(BANKS):
-            dst = out_slice(0, i)
+        for i, (nt, mt) in enumerate(BANKS_A):
+            dst = out_a[mt][:, N_TILE * nt : N_TILE * (nt + 1)]
             if i % 2 == 1:
                 nc.scalar.copy(out=dst, in_=acc[(nt, mt)][:])
                 later.append((dst, N_TILE * nt))
@@ -196,23 +200,27 @@ def tile_fp8amperelinear_kernel(tc, x, weight_words, weight_scales, bias, out):
             add_bias(dst, dst, n0)
 
         acc = {}
-        for b in BANKS:
+        for b in BANKS_B:
             acc[b] = psum.tile([P, N_TILE], F32, name="acc", tag="bank")
         for g in range(GROUPS - 2):
-            for nt, mt in BANKS:
+            for nt, mt in BANKS_B:
                 mx_pass(1, g, acc, nt, mt)
-        for i, (nt, mt) in enumerate(BANKS):
+        for i, (nt, mt) in enumerate(BANKS_B):
             mx_pass(1, GROUPS - 2, acc, nt, mt)
             mx_pass(1, GROUPS - 1, acc, nt, mt)
-            add_bias(out_slice(1, i), acc[(nt, mt)][:], ROUND_COLS + N_TILE * nt)
+            if i < 4:
+                dst = out_b[i // 2][:, N_TILE * (i % 2) : N_TILE * (i % 2 + 1)]
+            else:
+                dst = out_b[i - 2][:]
+            add_bias(dst, acc[(nt, mt)][:], ROUND_COLS + N_TILE * nt)
 
         for mt in range(M_TILES):
             nc.sync.dma_start(out=out[P * mt : P * (mt + 1), 0:2048], in_=out_a[mt][:])
-        for pair in range(3):
-            nt, mt = BANKS[2 * pair]
+        for mt in range(M_TILES):
+            nc.sync.dma_start(
+                out=out[P * mt : P * (mt + 1), ROUND_COLS : ROUND_COLS + 1024], in_=out_b[mt][:]
+            )
+        for i in range(4, 8):
+            nt, mt = BANKS_B[i]
             c0 = ROUND_COLS + N_TILE * nt
-            nc.sync.dma_start(out=out[P * mt : P * (mt + 1), c0 : c0 + 1024], in_=out_b[pair][:])
-        for i in (6, 7):
-            nt, mt = BANKS[i]
-            c0 = ROUND_COLS + N_TILE * nt
-            nc.sync.dma_start(out=out[P * mt : P * (mt + 1), c0 : c0 + N_TILE], in_=out_b[i - 3][:])
+            nc.sync.dma_start(out=out[P * mt : P * (mt + 1), c0 : c0 + N_TILE], in_=out_b[i - 2][:])

@@ -34,9 +34,12 @@ def tile_fp8amperelinear_kernel(tc, x, weight_words, weight_scales, bias, out):
         keep = ctx.enter_context(tc.tile_pool(name="keep", bufs=1))
         psum = ctx.enter_context(tc.psum_pool(name="psum", bufs=8))
 
-        wplane = [keep.tile([P, N], U8, name="wplane%d" % h, align_bytes=256) for h in range(2)]
-        for h in range(2):
-            nc.vector.memset(wplane[h][:].bitcast(I32), 0)
+        wplane = {}
+        for h, r in ((0, 0), (1, 0), (0, 1), (1, 1)):
+            wplane[(h, r)] = keep.tile(
+                [P, ROUND_COLS], U8, name="wplane_%d_%d" % (h, r), align_bytes=256
+            )
+            nc.vector.memset(wplane[(h, r)][:].bitcast(I32), 0)
         ident_f = keep.tile([P, P], F32, name="ident_f")
         make_identity(nc, ident_f[:])
         ident_b = keep.tile([P, P], BF16, name="ident_b")
@@ -47,6 +50,16 @@ def tile_fp8amperelinear_kernel(tc, x, weight_words, weight_scales, bias, out):
             out=bias8[:],
             in_=bias.rearrange("(o j c) -> o j c", o=1, j=8).to_broadcast([16, 8, N_TILE]),
         )
+
+        def load_scales(queue, view, h, r):
+            c0 = ROUND_COLS * r
+            for q in range(4):
+                queue.dma_start(
+                    out=wplane[(h, r)][32 * q : 32 * q + 16, :].bitcast(view),
+                    in_=weight_scales[
+                        4 * h : 4 * h + 4, 4 * q : 4 * q + 4, c0 : c0 + ROUND_COLS
+                    ].bitcast(view),
+                )
 
         x_sb = [[None, None], [None, None]]
         for kh in range(2):
@@ -60,13 +73,12 @@ def tile_fp8amperelinear_kernel(tc, x, weight_words, weight_scales, bias, out):
                         in_=x[P * mt : P * (mt + 1), 2048 * kh + w * c : 2048 * kh + w * (c + 1)],
                     )
                 x_sb[mt][kh] = t
+                if (kh, mt) == (0, 0):
+                    load_scales(nc.sync, I32, 0, 0)
 
-        for h in range(2):
-            for q in range(4):
-                nc.gpsimd.dma_start(
-                    out=wplane[h][32 * q : 32 * q + 16, :].bitcast(F32),
-                    in_=weight_scales[4 * h : 4 * h + 4, 4 * q : 4 * q + 4, :].bitcast(F32),
-                )
+        load_scales(nc.gpsimd, F32, 1, 0)
+        load_scales(nc.gpsimd, F32, 0, 1)
+        load_scales(nc.gpsimd, F32, 1, 1)
 
         ww = weight_words.rearrange("g p n t -> g p (n t)")
         w_sb = {}
@@ -82,7 +94,9 @@ def tile_fp8amperelinear_kernel(tc, x, weight_words, weight_scales, bias, out):
             for i in range(count):
                 w_sb[(r, g, first + i)] = (t, N_TILE * i)
 
-        for g in range(GROUPS):
+        load_w(0, 0, 0, 2)
+        load_w(0, 0, 2, 2)
+        for g in range(1, GROUPS):
             load_w(0, g, 0, 4)
         for g in range(GROUPS - 2):
             load_w(1, g, 0, 4)
@@ -167,14 +181,13 @@ def tile_fp8amperelinear_kernel(tc, x, weight_words, weight_scales, bias, out):
 
         def mx_pass(r, g, acc, nt, mt):
             h, k = g // 4, g % 4
-            n0 = ROUND_COLS * r + N_TILE * nt
             t, c = w_sb[(r, g, nt)]
             nc.tensor.matmul_mx(
                 out=acc[(nt, mt)][:],
                 lhsT=codes_of(g, mt),
                 lhsT_scale=plane_of(g, mt),
                 rhs=t[:, c : c + N_TILE].bitcast(FP8X4),
-                rhs_scale=wplane[h][4 * k : P, n0 : n0 + N_TILE],
+                rhs_scale=wplane[(h, r)][4 * k : P, N_TILE * nt : N_TILE * (nt + 1)],
                 start=(g == 0),
                 stop=(g == GROUPS - 1),
             )

@@ -20,7 +20,6 @@ K = 4096
 N = 4096
 N_TILE = 512
 ROUND_COLS = 2048
-PAD = 48
 
 BANKS_A = [(0, 0), (1, 0), (0, 1), (1, 1), (2, 0), (3, 0), (2, 1), (3, 1)]
 BANKS_B = [(0, 0), (1, 0), (0, 1), (1, 1), (2, 0), (2, 1), (3, 0), (3, 1)]
@@ -37,7 +36,7 @@ def tile_fp8amperelinear_kernel(tc, x, weight_words, weight_scales, bias, out):
         wplane = {}
         for h, r in ((0, 0), (1, 0), (0, 1), (1, 1)):
             wplane[(h, r)] = keep.tile(
-                [P, ROUND_COLS], U8, name="wplane_%d_%d" % (h, r), align_bytes=256
+                [P, ROUND_COLS], U8, name="wplane_%d_%d" % (h, r), align_bytes=64
             )
             nc.vector.memset(wplane[(h, r)][:].bitcast(I32), 0)
         ident_f = keep.tile([P, P], F32, name="ident_f")
@@ -85,7 +84,7 @@ def tile_fp8amperelinear_kernel(tc, x, weight_words, weight_scales, bias, out):
 
         def load_w(r, g, first, count):
             t = keep.tile(
-                [P, N_TILE * count], U32, name="w_sb_%d_%d_%d" % (r, g, first), align_bytes=256
+                [P, N_TILE * count], U32, name="w_sb_%d_%d_%d" % (r, g, first), align_bytes=64
             )
             c0 = 4 * (ROUND_COLS * r + N_TILE * first)
             nc.sync.dma_start(
@@ -105,25 +104,25 @@ def tile_fp8amperelinear_kernel(tc, x, weight_words, weight_scales, bias, out):
                 load_w(1, g, first, count)
 
         bias_bc = keep.tile([P, N], BF16, name="bias_bc")
-        xcodes = keep.tile([P, PAD + GROUPS * 256], U32, name="xcodes", align_bytes=256)
-        xplane = keep.tile([P, 2 * GROUPS, 256], U8, name="xplane", align_bytes=256)
+        xcodes = keep.tile([P, GROUPS, 256], U32, name="xcodes", align_bytes=64)
+        xplane = keep.tile([P, GROUPS, 256], U8, name="xplane", align_bytes=64)
         grouped = [
             keep.tile([P, 2048], BF16, name="grouped%d" % j, align_bytes=64) for j in range(4)
         ]
 
         def codes_of(g, mt):
-            o = PAD + 256 * g + P * mt
-            return xcodes[:, o : o + P].bitcast(FP8X4)
+            return xcodes[:, g, P * mt : P * (mt + 1)].bitcast(FP8X4)
 
         def plane_of(g, mt):
-            return xplane[:, 2 * g + mt, 0:P]
+            return xplane[:, g, P * mt : P * (mt + 1)]
 
         def quantise(g):
-            for mt in range(M_TILES):
-                o = 1024 * (g % 2) + 512 * mt
-                nc.vector.quantize_mx(
-                    out=codes_of(g, mt), scales=plane_of(g, mt), in_=grouped[g // 2][:, o : o + 512]
-                )
+            o = 1024 * (g % 2)
+            nc.vector.quantize_mx(
+                out=xcodes[:, g, :].bitcast(FP8X4),
+                scales=xplane[:, g, :],
+                in_=grouped[g // 2][:, o : o + 1024],
+            )
 
         def spread_bias(i):
             pb = psum.tile([P, 1024], BF16, name="pb", tag="bank")

@@ -20,6 +20,7 @@ K = 4096
 N = 4096
 N_TILE = 512
 ROUND_COLS = 2048
+PAD = 48
 
 BANKS_A = [(0, 0), (1, 0), (0, 1), (1, 1), (2, 0), (3, 0), (2, 1), (3, 1)]
 BANKS_B = [(0, 0), (1, 0), (0, 1), (1, 1), (2, 0), (2, 1), (3, 0), (3, 1)]
@@ -36,7 +37,7 @@ def tile_fp8amperelinear_kernel(tc, x, weight_words, weight_scales, bias, out):
         wplane = {}
         for h, r in ((0, 0), (1, 0), (0, 1), (1, 1)):
             wplane[(h, r)] = keep.tile(
-                [P, ROUND_COLS], U8, name="wplane_%d_%d" % (h, r), align_bytes=64
+                [P, ROUND_COLS], U8, name="wplane_%d_%d" % (h, r), align_bytes=256
             )
             nc.vector.memset(wplane[(h, r)][:].bitcast(I32), 0)
         ident_f = keep.tile([P, P], F32, name="ident_f")
@@ -72,9 +73,8 @@ def tile_fp8amperelinear_kernel(tc, x, weight_words, weight_scales, bias, out):
                         in_=x[P * mt : P * (mt + 1), 2048 * kh + w * c : 2048 * kh + w * (c + 1)],
                     )
                 x_sb[mt][kh] = t
-                if (kh, mt) == (0, 0):
-                    load_scales(nc.sync, I32, 0, 0)
 
+        load_scales(nc.sync, I32, 0, 0)
         load_scales(nc.gpsimd, F32, 1, 0)
         load_scales(nc.gpsimd, F32, 0, 1)
         load_scales(nc.gpsimd, F32, 1, 1)
@@ -84,7 +84,7 @@ def tile_fp8amperelinear_kernel(tc, x, weight_words, weight_scales, bias, out):
 
         def load_w(r, g, first, count):
             t = keep.tile(
-                [P, N_TILE * count], U32, name="w_sb_%d_%d_%d" % (r, g, first), align_bytes=64
+                [P, N_TILE * count], U32, name="w_sb_%d_%d_%d" % (r, g, first), align_bytes=256
             )
             c0 = 4 * (ROUND_COLS * r + N_TILE * first)
             nc.sync.dma_start(
@@ -104,25 +104,25 @@ def tile_fp8amperelinear_kernel(tc, x, weight_words, weight_scales, bias, out):
                 load_w(1, g, first, count)
 
         bias_bc = keep.tile([P, N], BF16, name="bias_bc")
-        xcodes = keep.tile([P, GROUPS, 256], U32, name="xcodes", align_bytes=64)
-        xplane = keep.tile([P, GROUPS, 256], U8, name="xplane", align_bytes=64)
+        xcodes = keep.tile([P, PAD + GROUPS * 256], U32, name="xcodes", align_bytes=256)
+        xplane = keep.tile([P, 2 * GROUPS, 256], U8, name="xplane", align_bytes=256)
         grouped = [
             keep.tile([P, 2048], BF16, name="grouped%d" % j, align_bytes=64) for j in range(4)
         ]
 
         def codes_of(g, mt):
-            return xcodes[:, g, P * mt : P * (mt + 1)].bitcast(FP8X4)
+            o = PAD + 256 * g + P * mt
+            return xcodes[:, o : o + P].bitcast(FP8X4)
 
         def plane_of(g, mt):
-            return xplane[:, g, P * mt : P * (mt + 1)]
+            return xplane[:, 2 * g + mt, 0:P]
 
         def quantise(g):
-            o = 1024 * (g % 2)
-            nc.vector.quantize_mx(
-                out=xcodes[:, g, :].bitcast(FP8X4),
-                scales=xplane[:, g, :],
-                in_=grouped[g // 2][:, o : o + 1024],
-            )
+            for mt in range(M_TILES):
+                o = 1024 * (g % 2) + 512 * mt
+                nc.vector.quantize_mx(
+                    out=codes_of(g, mt), scales=plane_of(g, mt), in_=grouped[g // 2][:, o : o + 512]
+                )
 
         def spread_bias(i):
             pb = psum.tile([P, 1024], BF16, name="pb", tag="bank")
@@ -148,33 +148,71 @@ def tile_fp8amperelinear_kernel(tc, x, weight_words, weight_scales, bias, out):
             )
             engine_copy(out=dst, in_=xt[:].rearrange("p u m -> p m u"))
 
-        for kh in range(2):
-            xt = [
+        xs = [
+            keep.tile([P, 2, 1024], F32, name="xs_%d" % mt, tag="big_%d" % mt)
+            for mt in range(M_TILES)
+        ]
+
+        def sort_words(kh, mt):
+            words = x_sb[mt][kh][:].bitcast(F32)
+            for half, engine_copy in ((0, nc.vector.tensor_copy), (1, nc.scalar.copy)):
+                cols = slice(512 * half, 512 * (half + 1))
+                engine_copy(
+                    out=xs[mt][:, kh, cols].rearrange("m (g u p) -> m g u p", g=2, u=2),
+                    in_=words[:, cols].rearrange("m (g p u) -> m g u p", g=2, u=2),
+                )
+
+        def transposes(kh, mt, xt):
+            for gl in range(4):
+                for u in range(2):
+                    o = 256 * gl + P * u
+                    nc.tensor.transpose(
+                        xt[gl][:, u, P * mt : P * (mt + 1)], xs[mt][:, kh, o : o + P], ident_f[:]
+                    )
+
+        def banks_for_x(kh):
+            return [
                 psum.tile([P, 2, 256], F32, name="xt%d" % (4 * kh + gl), tag="bank")
                 for gl in range(4)
             ]
-            pbs = []
-            for mt in range(M_TILES):
-                words = x_sb[mt][kh][:].bitcast(F32)
-                for gl in range(4):
-                    for u in range(2):
-                        nc.tensor.transpose(
-                            xt[gl][:, u, P * mt : P * (mt + 1)],
-                            words[:, 256 * gl + u : 256 * (gl + 1) : 2],
-                            ident_f[:],
-                        )
-                pbs.append(spread_bias(2 * kh + mt))
-            g0 = 4 * kh
-            bias_out(2 * kh, pbs[0])
-            regroup(g0 + 0, xt[0], nc.vector.tensor_copy)
-            regroup(g0 + 1, xt[1], nc.scalar.copy)
-            regroup(g0 + 2, xt[2], nc.vector.tensor_copy)
-            regroup(g0 + 3, xt[3], nc.scalar.copy)
-            bias_out(2 * kh + 1, pbs[1])
-            for gl in range(4):
-                quantise(g0 + gl)
 
-        out_a = [keep.tile([P, 2048], F32, name="out_a_%d" % mt) for mt in range(M_TILES)]
+        xt = banks_for_x(0)
+        sort_words(0, 0)
+        transposes(0, 0, xt)
+        pb0 = spread_bias(0)
+        sort_words(0, 1)
+        bias_out(0, pb0)
+        transposes(0, 1, xt)
+        pb1 = spread_bias(1)
+        sort_words(1, 0)
+        regroup(0, xt[0], nc.vector.tensor_copy)
+        regroup(1, xt[1], nc.scalar.copy)
+        xu = banks_for_x(1)
+        transposes(1, 0, xu)
+        pb2 = spread_bias(2)
+        sort_words(1, 1)
+        quantise(0)
+        regroup(2, xt[2], nc.vector.tensor_copy)
+        regroup(3, xt[3], nc.scalar.copy)
+        quantise(1)
+        bias_out(1, pb1)
+        transposes(1, 1, xu)
+        pb3 = spread_bias(3)
+        regroup(4, xu[0], nc.vector.tensor_copy)
+        regroup(5, xu[1], nc.scalar.copy)
+        regroup(6, xu[2], nc.vector.tensor_copy)
+        regroup(7, xu[3], nc.scalar.copy)
+        quantise(2)
+        quantise(3)
+        bias_out(2, pb2)
+        bias_out(3, pb3)
+        for g in range(4, GROUPS):
+            quantise(g)
+
+        out_a = [
+            keep.tile([P, 2048], F32, name="out_a_%d" % mt, tag="big_%d" % mt)
+            for mt in range(M_TILES)
+        ]
         out_b = [keep.tile([P, 1024], F32, name="out_b_%d" % i) for i in range(2)]
         out_b.extend([keep.tile([P, N_TILE], F32, name="out_b_%d" % i) for i in range(2, 6)])
 

from contextlib import ExitStack

import concourse.mybir as mybir
from concourse.masks import make_identity

FLOPS = 2 * 256 * 4096 * 4096

F32 = mybir.dt.float32
BF16 = mybir.dt.bfloat16
I32 = mybir.dt.int32
U32 = mybir.dt.uint32
U8 = mybir.dt.uint8
FP8X4 = mybir.dt.float8_e4m3fn_x4
ADD = mybir.AluOpType.add

P = 128
M_TILES = 2
GROUPS = 8
K = 4096
N = 4096
N_TILE = 512
ROUND_COLS = 2048
PAD = 48

BANKS_A = [(0, 0), (1, 0), (0, 1), (1, 1), (2, 0), (3, 0), (2, 1), (3, 1)]
BANKS_B = [(0, 0), (1, 0), (0, 1), (1, 1), (2, 0), (2, 1), (3, 0), (3, 1)]
TAPER = [(0, 2), (2, 1), (3, 1)]


def tile_fp8amperelinear_kernel(tc, x, weight_words, weight_scales, bias, out):
    nc = tc.nc
    with ExitStack() as ctx:
        ctx.enter_context(tc.manual_schedule())
        keep = ctx.enter_context(tc.tile_pool(name="keep", bufs=1))
        psum = ctx.enter_context(tc.psum_pool(name="psum", bufs=8))

        wplane = {}
        for h, r in ((0, 0), (1, 0), (0, 1), (1, 1)):
            wplane[(h, r)] = keep.tile(
                [P, ROUND_COLS], U8, name="wplane_%d_%d" % (h, r), align_bytes=256
            )
            nc.vector.memset(wplane[(h, r)][:].bitcast(I32), 0)
        ident_f = keep.tile([P, P], F32, name="ident_f")
        make_identity(nc, ident_f[:])
        ident_b = keep.tile([P, P], BF16, name="ident_b")
        make_identity(nc, ident_b[:])

        bias8 = keep.tile([P, N_TILE], BF16, name="bias8")
        nc.scalar.dma_start(
            out=bias8[:],
            in_=bias.rearrange("(o j c) -> o j c", o=1, j=8).to_broadcast([16, 8, N_TILE]),
        )

        def load_scales(queue, view, h, r):
            c0 = ROUND_COLS * r
            for q in range(4):
                queue.dma_start(
                    out=wplane[(h, r)][32 * q : 32 * q + 16, :].bitcast(view),
                    in_=weight_scales[
                        4 * h : 4 * h + 4, 4 * q : 4 * q + 4, c0 : c0 + ROUND_COLS
                    ].bitcast(view),
                )

        x_sb = [[None, None], [None, None]]
        for kh in range(2):
            for mt in range(M_TILES):
                t = keep.tile([P, 2048], BF16, name="x_sb_%d_%d" % (mt, kh))
                cuts = 2 if (kh, mt) == (0, 0) else 1
                w = 2048 // cuts
                for c in range(cuts):
                    nc.sync.dma_start(
                        out=t[:, w * c : w * (c + 1)],
                        in_=x[P * mt : P * (mt + 1), 2048 * kh + w * c : 2048 * kh + w * (c + 1)],
                    )
                x_sb[mt][kh] = t

        load_scales(nc.sync, I32, 0, 0)
        load_scales(nc.gpsimd, F32, 1, 0)
        load_scales(nc.gpsimd, F32, 0, 1)
        load_scales(nc.gpsimd, F32, 1, 1)

        ww = weight_words.rearrange("g p n t -> g p (n t)")
        w_sb = {}

        def load_w(r, g, first, count):
            t = keep.tile(
                [P, N_TILE * count], U32, name="w_sb_%d_%d_%d" % (r, g, first), align_bytes=256
            )
            c0 = 4 * (ROUND_COLS * r + N_TILE * first)
            nc.sync.dma_start(
                out=t[:].bitcast(I32), in_=ww[g, :, c0 : c0 + 4 * N_TILE * count].bitcast(I32)
            )
            for i in range(count):
                w_sb[(r, g, first + i)] = (t, N_TILE * i)

        load_w(0, 0, 0, 2)
        load_w(0, 0, 2, 2)
        for g in range(1, GROUPS):
            load_w(0, g, 0, 4)
        for g in range(GROUPS - 2):
            load_w(1, g, 0, 4)
        for first, count in TAPER:
            for g in (GROUPS - 2, GROUPS - 1):
                load_w(1, g, first, count)

        bias_bc = keep.tile([P, N], BF16, name="bias_bc")
        xcodes = keep.tile([P, PAD + GROUPS * 256], U32, name="xcodes", align_bytes=256)
        xplane = keep.tile([P, 2 * GROUPS, 256], U8, name="xplane", align_bytes=256)
        grouped = [
            keep.tile([P, 2048], BF16, name="grouped%d" % j, align_bytes=64) for j in range(4)
        ]

        def codes_of(g, mt):
            o = PAD + 256 * g + P * mt
            return xcodes[:, o : o + P].bitcast(FP8X4)

        def plane_of(g, mt):
            return xplane[:, 2 * g + mt, 0:P]

        def quantise(g):
            for mt in range(M_TILES):
                o = 1024 * (g % 2) + 512 * mt
                nc.vector.quantize_mx(
                    out=codes_of(g, mt), scales=plane_of(g, mt), in_=grouped[g // 2][:, o : o + 512]
                )

        def spread_bias(i):
            pb = psum.tile([P, 1024], BF16, name="pb", tag="bank")
            for e in range(2):
                j = 2 * i + e
                nc.tensor.matmul(
                    pb[:, N_TILE * e : N_TILE * (e + 1)],
                    lhsT=ident_b[:, j : j + 1].to_broadcast([P, P]),
                    rhs=bias8[:],
                    start=True,
                    stop=True,
                )
            return pb

        def bias_out(i, pb):
            nc.scalar.copy(out=bias_bc[:, 1024 * i : 1024 * (i + 1)], in_=pb[:])

        def regroup(g, xt, engine_copy):
            dst = (
                grouped[g // 2][:, 1024 * (g % 2) : 1024 * (g % 2 + 1)]
                .bitcast(F32)
                .rearrange("p (m u) -> p m u", u=2)
            )
            engine_copy(out=dst, in_=xt[:].rearrange("p u m -> p m u"))

        xs = [
            keep.tile([P, 2, 1024], F32, name="xs_%d" % mt, tag="big_%d" % mt)
            for mt in range(M_TILES)
        ]

        def sort_words(kh, mt):
            words = x_sb[mt][kh][:].bitcast(F32)
            for half, engine_copy in ((0, nc.vector.tensor_copy), (1, nc.scalar.copy)):
                cols = slice(512 * half, 512 * (half + 1))
                engine_copy(
                    out=xs[mt][:, kh, cols].rearrange("m (g u p) -> m g u p", g=2, u=2),
                    in_=words[:, cols].rearrange("m (g p u) -> m g u p", g=2, u=2),
                )

        def transposes(kh, mt, xt):
            for gl in range(4):
                for u in range(2):
                    o = 256 * gl + P * u
                    nc.tensor.transpose(
                        xt[gl][:, u, P * mt : P * (mt + 1)], xs[mt][:, kh, o : o + P], ident_f[:]
                    )

        def banks_for_x(kh):
            return [
                psum.tile([P, 2, 256], F32, name="xt%d" % (4 * kh + gl), tag="bank")
                for gl in range(4)
            ]

        xt = banks_for_x(0)
        sort_words(0, 0)
        transposes(0, 0, xt)
        pb0 = spread_bias(0)
        sort_words(0, 1)
        bias_out(0, pb0)
        transposes(0, 1, xt)
        pb1 = spread_bias(1)
        sort_words(1, 0)
        regroup(0, xt[0], nc.vector.tensor_copy)
        regroup(1, xt[1], nc.scalar.copy)
        xu = banks_for_x(1)
        transposes(1, 0, xu)
        pb2 = spread_bias(2)
        sort_words(1, 1)
        quantise(0)
        regroup(2, xt[2], nc.vector.tensor_copy)
        regroup(3, xt[3], nc.scalar.copy)
        quantise(1)
        bias_out(1, pb1)
        transposes(1, 1, xu)
        pb3 = spread_bias(3)
        regroup(4, xu[0], nc.vector.tensor_copy)
        regroup(5, xu[1], nc.scalar.copy)
        regroup(6, xu[2], nc.vector.tensor_copy)
        regroup(7, xu[3], nc.scalar.copy)
        quantise(2)
        quantise(3)
        bias_out(2, pb2)
        bias_out(3, pb3)
        for g in range(4, GROUPS):
            quantise(g)

        out_a = [
            keep.tile([P, 2048], F32, name="out_a_%d" % mt, tag="big_%d" % mt)
            for mt in range(M_TILES)
        ]
        out_b = [keep.tile([P, 1024], F32, name="out_b_%d" % i) for i in range(2)]
        out_b.extend([keep.tile([P, N_TILE], F32, name="out_b_%d" % i) for i in range(2, 6)])

        def mx_pass(r, g, acc, nt, mt):
            h, k = g // 4, g % 4
            t, c = w_sb[(r, g, nt)]
            nc.tensor.matmul_mx(
                out=acc[(nt, mt)][:],
                lhsT=codes_of(g, mt),
                lhsT_scale=plane_of(g, mt),
                rhs=t[:, c : c + N_TILE].bitcast(FP8X4),
                rhs_scale=wplane[(h, r)][4 * k : P, N_TILE * nt : N_TILE * (nt + 1)],
                start=(g == 0),
                stop=(g == GROUPS - 1),
            )

        def add_bias(dst, src, n0):
            nc.vector.tensor_tensor(out=dst, in0=src, in1=bias_bc[:, n0 : n0 + N_TILE], op=ADD)

        acc = {}
        for b in BANKS_A:
            acc[b] = psum.tile([P, N_TILE], F32, name="acc", tag="bank")
        for g in range(GROUPS):
            for nt, mt in BANKS_A:
                mx_pass(0, g, acc, nt, mt)
        later = []
        for i, (nt, mt) in enumerate(BANKS_A):
            dst = out_a[mt][:, N_TILE * nt : N_TILE * (nt + 1)]
            if i % 2 == 1:
                nc.scalar.copy(out=dst, in_=acc[(nt, mt)][:])
                later.append((dst, N_TILE * nt))
            else:
                add_bias(dst, acc[(nt, mt)][:], N_TILE * nt)
        for dst, n0 in later:
            add_bias(dst, dst, n0)

        acc = {}
        for b in BANKS_B:
            acc[b] = psum.tile([P, N_TILE], F32, name="acc", tag="bank")
        for g in range(GROUPS - 2):
            for nt, mt in BANKS_B:
                mx_pass(1, g, acc, nt, mt)
        for i, (nt, mt) in enumerate(BANKS_B):
            mx_pass(1, GROUPS - 2, acc, nt, mt)
            mx_pass(1, GROUPS - 1, acc, nt, mt)
            if i < 4:
                dst = out_b[i // 2][:, N_TILE * (i % 2) : N_TILE * (i % 2 + 1)]
            else:
                dst = out_b[i - 2][:]
            add_bias(dst, acc[(nt, mt)][:], ROUND_COLS + N_TILE * nt)

        for mt in range(M_TILES):
            nc.sync.dma_start(out=out[P * mt : P * (mt + 1), 0:2048], in_=out_a[mt][:])
        for mt in range(M_TILES):
            nc.sync.dma_start(
                out=out[P * mt : P * (mt + 1), ROUND_COLS : ROUND_COLS + 1024], in_=out_b[mt][:]
            )
        for i in range(4, 8):
            nt, mt = BANKS_B[i]
            c0 = ROUND_COLS + N_TILE * nt
            nc.sync.dma_start(out=out[P * mt : P * (mt + 1), c0 : c0 + N_TILE], in_=out_b[i - 2][:])
